import numpy as np
import ml_dtypes


def mxq(x, axis, fmt="e4m3"):
    dtype, down = {"e4m3": (ml_dtypes.float8_e4m3fn, 7), "e5m2": (ml_dtypes.float8_e5m2, 14)}[fmt]
    v = np.moveaxis(np.asarray(x, np.float32).astype(ml_dtypes.bfloat16).astype(np.float64), axis, -1)
    blocks = v.reshape(v.shape[:-1] + (-1, 32))
    amax = np.abs(blocks).max(-1, keepdims=True)
    byte = np.maximum(np.where(amax > 0, np.frexp(amax)[1] - 1 + 127, 0) - down, 1)
    scale = np.exp2(byte - 127.0)
    codes = (blocks / scale).astype(np.float32).astype(dtype).astype(np.float64)
    return np.moveaxis((codes * scale).reshape(v.shape), -1, axis)


WIDE = False


def mx_kscale(k):
    if not WIDE:
        return np.ones(k)
    levels = np.array([10, -10, 5, -5, 0])
    a = np.random.permutation(np.resize(levels, k // 512 * 4)).reshape(k // 512, 4)
    idx = np.arange(k)
    return np.exp2(a[idx // 512, idx % 128 // 32])


BF16 = ml_dtypes.bfloat16


def bf(x):
    return np.asarray(x, np.float32).astype(BF16)


def f64(x):
    return np.asarray(x).astype(np.float64)


E2M1 = np.array([0.0, 0.5, 1.0, 1.5, 2.0, 3.0, 4.0, 6.0, -0.0, -0.5, -1.0, -1.5, -2.0, -3.0, -4.0, -6.0])


def pack_weight(w, fmt):
    k, n = w.shape
    w = f64(bf(w)).reshape(k // 32, 32, n)
    amax = np.abs(w).max(1)
    if fmt == "e4m3":
        byte = np.frexp(amax)[1] - 1 + 127 - 7
    else:
        mant, ex = np.frexp(amax / 6.0)
        byte = np.where(mant > 0.5, ex, ex - 1) + 127
    byte = np.clip(np.where(amax > 0, byte, 1), 1, 254)
    scaled = (w * np.exp2(127.0 - byte)[:, None, :]).reshape(k, n).astype(np.float32)
    by_word = np.ascontiguousarray(scaled.reshape(k // 512, 128, 4, n).transpose(0, 1, 3, 2))
    if fmt == "e4m3":
        words = by_word.astype(ml_dtypes.float8_e4m3fn).view(np.uint8)
    else:
        c = by_word.astype(ml_dtypes.float4_e2m1fn).view(np.uint8) & 0xF
        words = c[..., 0::2] | (c[..., 1::2] << 4)
    return np.ascontiguousarray(words), np.ascontiguousarray(byte.astype(np.uint8).reshape(k // 512, 16, n))


def unpack_weight(words, scales, fmt):
    g, p, n, _ = words.shape
    if fmt == "e4m3":
        vals = np.ascontiguousarray(words).view(ml_dtypes.float8_e4m3fn).astype(np.float64)
    else:
        nib = np.empty((g, p, n, 4), np.uint8)
        nib[..., 0::2] = words & 0xF
        nib[..., 1::2] = words >> 4
        vals = E2M1[nib]
    vals = vals * np.repeat(np.exp2(scales.astype(np.float64) - 127.0), 8, axis=1)[..., None]
    return vals.transpose(0, 1, 3, 2).reshape(g * 512, n)


B, IN_DIM, R_IN, R_OUT = 128, 2048, 2048, 2048
HIDDEN = R_IN + R_OUT
BASELINE_THRE = 0.1
BETA = 1.8
R_M = 3.0
DT = 1.0
FMT = "e4m3"


def sigmoid(v):
    return 1.0 / (1.0 + np.exp(-v))


def setup_inputs():
    s = mx_kscale(IN_DIM)
    x_t = bf(np.random.standard_normal((B, IN_DIM)) * s)
    spk_t = bf(np.random.random((B, HIDDEN)) < 0.3)
    mem_t_in = bf(np.random.standard_normal((B, R_IN)))
    b_t_in = bf(np.random.random((B, R_IN)))
    W_x2in = np.random.standard_normal((R_IN, IN_DIM)) / np.sqrt(IN_DIM) / s[None, :]
    b_x2in = bf(np.random.standard_normal(R_IN) * 0.5)
    W_rec4in = np.random.standard_normal((R_IN, R_IN)) * 1.5 / np.sqrt(R_IN)
    b_rec4in = bf(np.random.standard_normal(R_IN) * 0.5)
    W_out2in = np.random.standard_normal((R_IN, R_OUT)) * 1.5 / np.sqrt(R_OUT)
    b_out2in = bf(np.random.standard_normal(R_IN) * 0.5)
    tau_adp_in = bf(1.5 + 0.5 * np.random.standard_normal(R_IN))
    tau_m_in = bf(2.0 + 0.5 * np.random.standard_normal(R_IN))
    W_x2in_words, W_x2in_scales = pack_weight(np.ascontiguousarray(W_x2in.T), FMT)
    W_rec4in_words, W_rec4in_scales = pack_weight(np.ascontiguousarray(W_rec4in.T), FMT)
    W_out2in_words, W_out2in_scales = pack_weight(np.ascontiguousarray(W_out2in.T), FMT)
    return {
        "x_t": x_t,
        "spk_t": spk_t,
        "mem_t_in": mem_t_in,
        "b_t_in": b_t_in,
        "W_x2in_words": W_x2in_words,
        "W_x2in_scales": W_x2in_scales,
        "b_x2in": b_x2in,
        "W_rec4in_words": W_rec4in_words,
        "W_rec4in_scales": W_rec4in_scales,
        "b_rec4in": b_rec4in,
        "W_out2in_words": W_out2in_words,
        "W_out2in_scales": W_out2in_scales,
        "b_out2in": b_out2in,
        "tau_adp_in": tau_adp_in,
        "tau_m_in": tau_m_in,
    }


def reference(x_t, spk_t, mem_t_in, b_t_in, W_x2in_words, W_x2in_scales, b_x2in, W_rec4in_words, W_rec4in_scales, b_rec4in, W_out2in_words, W_out2in_scales, b_out2in, tau_adp_in, tau_m_in):
    spk = f64(spk_t)
    spk_out = spk[:, :R_OUT]
    spk_in = spk[:, R_OUT:]
    x = (mxq(f64(x_t), 1, "e4m3") @ unpack_weight(W_x2in_words, W_x2in_scales, FMT)) + f64(b_x2in)
    rec = (mxq(spk_in, 1, "e4m3") @ unpack_weight(W_rec4in_words, W_rec4in_scales, FMT)) + f64(b_rec4in)
    fbk = (mxq(spk_out, 1, "e4m3") @ unpack_weight(W_out2in_words, W_out2in_scales, FMT)) + f64(b_out2in)
    r_in_ = x + rec + fbk
    tau_m_s = sigmoid(f64(tau_m_in))
    tau_adp_s = sigmoid(f64(tau_adp_in))
    b = tau_adp_s * f64(b_t_in) + (1.0 - tau_adp_s) * spk_in
    new_thre = BASELINE_THRE + BETA * b
    mem = f64(mem_t_in) * tau_m_s + (1.0 - tau_m_s) * R_M * r_in_ - new_thre * spk_in * DT
    return mem

@@ -1,0 +1,193 @@
+from contextlib import ExitStack
+
+import concourse.mybir as mybir
+from concourse.masks import make_identity
+
+F32 = mybir.dt.float32
+BF16 = mybir.dt.bfloat16
+I32 = mybir.dt.int32
+U32 = mybir.dt.uint32
+U8 = mybir.dt.uint8
+FP8X4 = mybir.dt.float8_e4m3fn_x4
+ALU = mybir.AluOpType
+ACT = mybir.ActivationFunctionType
+
+P = 128
+PACK = 4
+K_PASS = P * PACK
+FEATURES = 2048
+NEURONS = 2048
+OPERANDS = 3
+GROUPS = FEATURES // K_PASS
+PASSES = OPERANDS * GROUPS
+BANK = 512
+BANKS = NEURONS // BANK
+WORDS = K_PASS // 2
+
+FLOPS = 2 * P * OPERANDS * FEATURES * NEURONS
+
+
+def tile_snnlayer_pa_kernel(
+    tc,
+    x_t,
+    spk_t,
+    mem_t_in,
+    b_t_in,
+    W_x2in_words,
+    W_x2in_scales,
+    b_x2in,
+    W_rec4in_words,
+    W_rec4in_scales,
+    b_rec4in,
+    W_out2in_words,
+    W_out2in_scales,
+    b_out2in,
+    tau_adp_in,
+    tau_m_in,
+    out,
+):
+    nc = tc.nc
+    weight_words = (W_x2in_words, W_out2in_words, W_rec4in_words)
+    weight_scales = (W_x2in_scales, W_out2in_scales, W_rec4in_scales)
+
+    with ExitStack() as ctx:
+        keep = ctx.enter_context(tc.tile_pool(name="keep", bufs=1))
+        acc_pool = ctx.enter_context(tc.psum_pool(name="acc", bufs=1))
+        bank_pool = ctx.enter_context(tc.psum_pool(name="bank", bufs=4))
+
+        acts = keep.tile([P, PASSES * K_PASS], BF16)
+        nc.sync.dma_start(out=acts[:, 0:FEATURES], in_=x_t)
+        nc.sync.dma_start(out=acts[:, FEATURES : 3 * FEATURES], in_=spk_t)
+        spk_in = acts[:, 2 * FEATURES : 3 * FEATURES]
+
+        w_planes = keep.tile([P, OPERANDS, NEURONS], U8, align_bytes=64)
+        nc.vector.memset(w_planes[:].bitcast(I32), 0)
+        for o in range(OPERANDS):
+            for quad in range(4):
+                nc.sync.dma_start(
+                    out=w_planes[32 * quad : 32 * quad + 16, o, :].bitcast(I32),
+                    in_=weight_scales[o][:, 4 * quad : 4 * quad + 4, :].bitcast(I32),
+                )
+
+        b_last = keep.tile([P, NEURONS], BF16)
+        nc.sync.dma_start(out=b_last[:], in_=b_t_in)
+        mem_last = keep.tile([P, NEURONS], BF16)
+        nc.sync.dma_start(out=mem_last[:], in_=mem_t_in)
+
+        vec_rows = keep.tile([P, NEURONS], BF16)
+        nc.vector.memset(vec_rows[:], 0.0)
+        nc.gpsimd.dma_start(out=vec_rows[0:1, :], in_=tau_m_in.unsqueeze(0))
+        nc.gpsimd.dma_start(out=vec_rows[32:33, :], in_=tau_adp_in.unsqueeze(0))
+        nc.gpsimd.dma_start(out=vec_rows[64:65, :], in_=b_x2in.unsqueeze(0))
+        nc.gpsimd.dma_start(out=vec_rows[65:66, :], in_=b_rec4in.unsqueeze(0))
+        nc.gpsimd.dma_start(out=vec_rows[66:67, :], in_=b_out2in.unsqueeze(0))
+        pick = keep.tile([P, 3, P], BF16)
+        nc.vector.memset(pick[:], 0.0)
+        nc.vector.memset(pick[0:32, 0, :], 1.0)
+        nc.vector.memset(pick[32:64, 1, :], 1.0)
+        nc.vector.memset(pick[64:128, 2, :], 1.0)
+
+        w_words = []
+        for c in range(PASSES):
+            w_words.append(keep.tile([P, NEURONS], U32, name="w_words_%d" % c, align_bytes=64))
+
+        def load_weight_words(c, first, width):
+            source = weight_words[c // GROUPS][c % GROUPS].rearrange("p n t -> p (n t)")
+            nc.sync.dma_start(
+                out=w_words[c][:, first : first + width].bitcast(I32),
+                in_=source[:, PACK * first : PACK * (first + width)].bitcast(I32),
+            )
+
+        for c in range(PASSES - 1):
+            load_weight_words(c, 0, NEURONS)
+        for j in range(BANKS):
+            load_weight_words(PASSES - 1, j * BANK, BANK)
+
+        ident = keep.tile([P, P], F32)
+        make_identity(nc, ident[:])
+        act_words = acts[:].bitcast(F32)
+        grouped = keep.tile([P, PASSES, P, PACK], BF16, align_bytes=64)
+        grouped_words = grouped[:].bitcast(F32)
+        act_codes = keep.tile([P, PASSES * P], U32, align_bytes=64)
+        act_planes = keep.tile([P, PASSES * P], U8, align_bytes=64)
+        for pair in range(PASSES // 2):
+            flipped = bank_pool.tile([P, 2, 2, P], F32, tag="bank")
+            for h in range(2):
+                c = 2 * pair + h
+                for u in range(2):
+                    nc.tensor.transpose(
+                        flipped[:, h, u, :],
+                        act_words[:, c * WORDS + u : (c + 1) * WORDS : 2],
+                        ident[:],
+                    )
+            target = grouped_words[:, 2 * pair : 2 * pair + 2, :, :]
+            source = flipped[:].rearrange("p h u b -> p h b u")
+            if pair % 2 == 0:
+                nc.vector.tensor_copy(out=target, in_=source)
+            else:
+                nc.scalar.copy(out=target, in_=source)
+        for o in range(OPERANDS):
+            cols = slice(o * GROUPS * P, (o + 1) * GROUPS * P)
+            nc.vector.quantize_mx(
+                out=act_codes[:, cols].bitcast(FP8X4),
+                scales=act_planes[:, cols],
+                in_=grouped[:, o * GROUPS : (o + 1) * GROUPS, :, :].rearrange("p g b t -> p (g b t)"),
+            )
+
+        decay = keep.tile([P, NEURONS], F32)
+        leak = keep.tile([P, NEURONS], F32)
+        adapt = keep.tile([P, NEURONS], F32)
+        rest = keep.tile([P, NEURONS], F32)
+        for v in range(3):
+            for j in range(BANKS):
+                cols = slice(j * BANK, (j + 1) * BANK)
+                spread = bank_pool.tile([P, BANK], F32, tag="bank")
+                nc.tensor.matmul(spread[:], lhsT=pick[:, v, :], rhs=vec_rows[:, cols], start=True, stop=True)
+                if v == 0:
+                    nc.scalar.activation(out=decay[:, cols], in_=spread[:], func=ACT.Sigmoid)
+                    nc.scalar.activation(out=leak[:, cols], in_=spread[:], func=ACT.Sigmoid, scale=-1.0)
+                elif v == 1:
+                    nc.scalar.activation(out=adapt[:, cols], in_=spread[:], func=ACT.Sigmoid)
+                else:
+                    nc.vector.scalar_tensor_tensor(
+                        out=rest[:, cols], in0=spread[:], scalar=3.0, in1=leak[:, cols], op0=ALU.mult, op1=ALU.mult
+                    )
+
+        spk_part = keep.tile([P, NEURONS], F32)
+        nc.scalar.activation(out=spk_part[:], in_=spk_in, func=ACT.Copy, bias=0.1, scale=1.8)
+        thre = keep.tile([P, NEURONS], F32)
+        nc.vector.tensor_tensor(out=thre[:], in0=b_last[:], in1=spk_in, op=ALU.subtract)
+        nc.vector.tensor_tensor(out=thre[:], in0=thre[:], in1=adapt[:], op=ALU.mult)
+        nc.vector.scalar_tensor_tensor(
+            out=thre[:], in0=thre[:], scalar=1.8, in1=spk_part[:], op0=ALU.mult, op1=ALU.add
+        )
+        nc.vector.tensor_tensor(out=thre[:], in0=thre[:], in1=spk_in, op=ALU.mult)
+        kept = keep.tile([P, NEURONS], F32)
+        nc.vector.tensor_tensor(out=kept[:], in0=mem_last[:], in1=decay[:], op=ALU.mult)
+        nc.vector.tensor_tensor(out=kept[:], in0=kept[:], in1=thre[:], op=ALU.subtract)
+        nc.vector.tensor_tensor(out=rest[:], in0=rest[:], in1=kept[:], op=ALU.add)
+
+        acc = []
+        for j in range(BANKS):
+            acc.append(acc_pool.tile([P, BANK], F32, name="acc_%d" % j))
+        mem = keep.tile([P, NEURONS], F32)
+        for c in range(PASSES):
+            o = c // GROUPS
+            g = c % GROUPS
+            for j in range(BANKS):
+                cols = slice(j * BANK, (j + 1) * BANK)
+                nc.tensor.matmul_mx(
+                    out=acc[j][:],
+                    lhsT=act_codes[:, c * P : (c + 1) * P].bitcast(FP8X4),
+                    lhsT_scale=act_planes[:, c * P : (c + 1) * P],
+                    rhs=w_words[c][:, cols].bitcast(FP8X4),
+                    rhs_scale=w_planes[PACK * g : P, o, cols],
+                    start=(c == 0),
+                    stop=(c == PASSES - 1),
+                )
+                if c == PASSES - 1:
+                    nc.vector.scalar_tensor_tensor(
+                        out=mem[:, cols], in0=acc[j][:], scalar=3.0, in1=leak[:, cols], op0=ALU.mult, op1=ALU.mult
+                    )
+                    nc.vector.tensor_tensor(out=mem[:, cols], in0=mem[:, cols], in1=rest[:, cols], op=ALU.add)
+                    nc.sync.dma_start(out=out[:, cols], in_=mem[:, cols])

@@ -23,6 +23,10 @@ PASSES = OPERANDS * GROUPS
 BANK = 512
 BANKS = NEURONS // BANK
 WORDS = K_PASS // 2
+TAPER = 3
+SMALL_PER_LARGE = 2
+
+TAU_M, TAU_ADP, BIAS = 0, 1, 2
 
 FLOPS = 2 * P * OPERANDS * FEATURES * NEURONS
 
@@ -49,59 +53,71 @@ def tile_snnlayer_pa_kernel(
     nc = tc.nc
     weight_words = (W_x2in_words, W_out2in_words, W_rec4in_words)
     weight_scales = (W_x2in_scales, W_out2in_scales, W_rec4in_scales)
+    bank_cols = [slice(j * BANK, (j + 1) * BANK) for j in range(BANKS)]
 
     with ExitStack() as ctx:
         keep = ctx.enter_context(tc.tile_pool(name="keep", bufs=1))
         acc_pool = ctx.enter_context(tc.psum_pool(name="acc", bufs=1))
         bank_pool = ctx.enter_context(tc.psum_pool(name="bank", bufs=4))
 
-        acts = keep.tile([P, PASSES * K_PASS], BF16)
-        nc.sync.dma_start(out=acts[:, 0:FEATURES], in_=x_t)
-        nc.sync.dma_start(out=acts[:, FEATURES : 3 * FEATURES], in_=spk_t)
-        spk_in = acts[:, 2 * FEATURES : 3 * FEATURES]
+        small_loads = []
+        large_loads = []
+
+        vec_rows = keep.tile([P, NEURONS], BF16)
+        nc.vector.memset(vec_rows[:], 0.0)
+        small_loads.append((vec_rows[32:33, :], tau_adp_in.unsqueeze(0)))
+        small_loads.append((vec_rows[0:1, :], tau_m_in.unsqueeze(0)))
+        small_loads.append((vec_rows[64:65, :], b_x2in.unsqueeze(0)))
+        small_loads.append((vec_rows[65:66, :], b_rec4in.unsqueeze(0)))
+        small_loads.append((vec_rows[66:67, :], b_out2in.unsqueeze(0)))
 
         w_planes = keep.tile([P, OPERANDS, NEURONS], U8, align_bytes=64)
         nc.vector.memset(w_planes[:].bitcast(I32), 0)
         for o in range(OPERANDS):
             for quad in range(4):
-                nc.sync.dma_start(
-                    out=w_planes[32 * quad : 32 * quad + 16, o, :].bitcast(I32),
-                    in_=weight_scales[o][:, 4 * quad : 4 * quad + 4, :].bitcast(I32),
+                small_loads.append(
+                    (
+                        w_planes[32 * quad : 32 * quad + 16, o, :].bitcast(I32),
+                        weight_scales[o][:, 4 * quad : 4 * quad + 4, :].bitcast(I32),
+                    )
                 )
 
+        acts = keep.tile([P, PASSES * K_PASS], BF16)
+        spk_in = acts[:, 2 * FEATURES : 3 * FEATURES]
         b_last = keep.tile([P, NEURONS], BF16)
-        nc.sync.dma_start(out=b_last[:], in_=b_t_in)
         mem_last = keep.tile([P, NEURONS], BF16)
-        nc.sync.dma_start(out=mem_last[:], in_=mem_t_in)
-
-        vec_rows = keep.tile([P, NEURONS], BF16)
-        nc.vector.memset(vec_rows[:], 0.0)
-        nc.gpsimd.dma_start(out=vec_rows[0:1, :], in_=tau_m_in.unsqueeze(0))
-        nc.gpsimd.dma_start(out=vec_rows[32:33, :], in_=tau_adp_in.unsqueeze(0))
-        nc.gpsimd.dma_start(out=vec_rows[64:65, :], in_=b_x2in.unsqueeze(0))
-        nc.gpsimd.dma_start(out=vec_rows[65:66, :], in_=b_rec4in.unsqueeze(0))
-        nc.gpsimd.dma_start(out=vec_rows[66:67, :], in_=b_out2in.unsqueeze(0))
-        pick = keep.tile([P, 3, P], BF16)
-        nc.vector.memset(pick[:], 0.0)
-        nc.vector.memset(pick[0:32, 0, :], 1.0)
-        nc.vector.memset(pick[32:64, 1, :], 1.0)
-        nc.vector.memset(pick[64:128, 2, :], 1.0)
+        large_loads.append((acts[:, 0:FEATURES], x_t))
+        large_loads.append((acts[:, FEATURES : 3 * FEATURES], spk_t))
+        large_loads.append((b_last[:], b_t_in))
+        large_loads.append((mem_last[:], mem_t_in))
 
         w_words = []
         for c in range(PASSES):
             w_words.append(keep.tile([P, NEURONS], U32, name="w_words_%d" % c, align_bytes=64))
 
-        def load_weight_words(c, first, width):
+        def weight_load(c, first, width):
             source = weight_words[c // GROUPS][c % GROUPS].rearrange("p n t -> p (n t)")
-            nc.sync.dma_start(
-                out=w_words[c][:, first : first + width].bitcast(I32),
-                in_=source[:, PACK * first : PACK * (first + width)].bitcast(I32),
+            return (
+                w_words[c][:, first : first + width].bitcast(I32),
+                source[:, PACK * first : PACK * (first + width)].bitcast(I32),
             )
 
-        for c in range(PASSES - 1):
-            load_weight_words(c, 0, NEURONS)
+        for c in range(PASSES - TAPER):
+            large_loads.append(weight_load(c, 0, NEURONS))
         for j in range(BANKS):
-            load_weight_words(PASSES - 1, j * BANK, BANK)
+            for c in range(PASSES - TAPER, PASSES):
+                large_loads.append(weight_load(c, j * BANK, BANK))
+
+        for i, (destination, source) in enumerate(large_loads):
+            nc.sync.dma_start(out=destination, in_=source)
+            for small_destination, small_source in small_loads[SMALL_PER_LARGE * i : SMALL_PER_LARGE * (i + 1)]:
+                nc.sync.dma_start(out=small_destination, in_=small_source)
+
+        pick = keep.tile([P, 3, P], BF16)
+        nc.vector.memset(pick[:], 0.0)
+        nc.vector.memset(pick[0:32, TAU_M, :], 1.0)
+        nc.vector.memset(pick[32:64, TAU_ADP, :], 1.0)
+        nc.vector.memset(pick[64:128, BIAS, :], 1.0)
 
         ident = keep.tile([P, P], F32)
         make_identity(nc, ident[:])
@@ -121,11 +137,11 @@ def tile_snnlayer_pa_kernel(
                         ident[:],
                     )
             target = grouped_words[:, 2 * pair : 2 * pair + 2, :, :]
-            source = flipped[:].rearrange("p h u b -> p h b u")
+            permuted = flipped[:].rearrange("p h u b -> p h b u")
             if pair % 2 == 0:
-                nc.vector.tensor_copy(out=target, in_=source)
+                nc.vector.tensor_copy(out=target, in_=permuted)
             else:
-                nc.scalar.copy(out=target, in_=source)
+                nc.scalar.copy(out=target, in_=permuted)
         for o in range(OPERANDS):
             cols = slice(o * GROUPS * P, (o + 1) * GROUPS * P)
             nc.vector.quantize_mx(
@@ -134,27 +150,23 @@ def tile_snnlayer_pa_kernel(
                 in_=grouped[:, o * GROUPS : (o + 1) * GROUPS, :, :].rearrange("p g b t -> p (g b t)"),
             )
 
-        decay = keep.tile([P, NEURONS], F32)
-        leak = keep.tile([P, NEURONS], F32)
-        adapt = keep.tile([P, NEURONS], F32)
-        rest = keep.tile([P, NEURONS], F32)
-        for v in range(3):
-            for j in range(BANKS):
-                cols = slice(j * BANK, (j + 1) * BANK)
-                spread = bank_pool.tile([P, BANK], F32, tag="bank")
-                nc.tensor.matmul(spread[:], lhsT=pick[:, v, :], rhs=vec_rows[:, cols], start=True, stop=True)
-                if v == 0:
-                    nc.scalar.activation(out=decay[:, cols], in_=spread[:], func=ACT.Sigmoid)
-                    nc.scalar.activation(out=leak[:, cols], in_=spread[:], func=ACT.Sigmoid, scale=-1.0)
-                elif v == 1:
-                    nc.scalar.activation(out=adapt[:, cols], in_=spread[:], func=ACT.Sigmoid)
-                else:
-                    nc.vector.scalar_tensor_tensor(
-                        out=rest[:, cols], in0=spread[:], scalar=3.0, in1=leak[:, cols], op0=ALU.mult, op1=ALU.mult
-                    )
+        def spread_vector(v, cols):
+            spread = bank_pool.tile([P, BANK], F32, tag="bank")
+            nc.tensor.matmul(spread[:], lhsT=pick[:, v, :], rhs=vec_rows[:, cols], start=True, stop=True)
+            return spread
 
+        adapt = keep.tile([P, NEURONS], F32)
+        for cols in bank_cols:
+            nc.scalar.activation(out=adapt[:, cols], in_=spread_vector(TAU_ADP, cols)[:], func=ACT.Sigmoid)
         spk_part = keep.tile([P, NEURONS], F32)
         nc.scalar.activation(out=spk_part[:], in_=spk_in, func=ACT.Copy, bias=0.1, scale=1.8)
+        decay = keep.tile([P, NEURONS], F32)
+        leak = keep.tile([P, NEURONS], F32)
+        for cols in bank_cols:
+            tau = spread_vector(TAU_M, cols)
+            nc.scalar.activation(out=decay[:, cols], in_=tau[:], func=ACT.Sigmoid)
+            nc.scalar.activation(out=leak[:, cols], in_=tau[:], func=ACT.Sigmoid, scale=-1.0)
+
         thre = keep.tile([P, NEURONS], F32)
         nc.vector.tensor_tensor(out=thre[:], in0=b_last[:], in1=spk_in, op=ALU.subtract)
         nc.vector.tensor_tensor(out=thre[:], in0=thre[:], in1=adapt[:], op=ALU.mult)
@@ -165,29 +177,43 @@ def tile_snnlayer_pa_kernel(
         kept = keep.tile([P, NEURONS], F32)
         nc.vector.tensor_tensor(out=kept[:], in0=mem_last[:], in1=decay[:], op=ALU.mult)
         nc.vector.tensor_tensor(out=kept[:], in0=kept[:], in1=thre[:], op=ALU.subtract)
+        rest = keep.tile([P, NEURONS], F32)
+        for cols in bank_cols:
+            nc.vector.scalar_tensor_tensor(
+                out=rest[:, cols],
+                in0=spread_vector(BIAS, cols)[:],
+                scalar=3.0,
+                in1=leak[:, cols],
+                op0=ALU.mult,
+                op1=ALU.mult,
+            )
         nc.vector.tensor_tensor(out=rest[:], in0=rest[:], in1=kept[:], op=ALU.add)
 
         acc = []
         for j in range(BANKS):
             acc.append(acc_pool.tile([P, BANK], F32, name="acc_%d" % j))
-        mem = keep.tile([P, NEURONS], F32)
-        for c in range(PASSES):
-            o = c // GROUPS
-            g = c % GROUPS
+
+        def mx_pass(c, j):
+            nc.tensor.matmul_mx(
+                out=acc[j][:],
+                lhsT=act_codes[:, c * P : (c + 1) * P].bitcast(FP8X4),
+                lhsT_scale=act_planes[:, c * P : (c + 1) * P],
+                rhs=w_words[c][:, bank_cols[j]].bitcast(FP8X4),
+                rhs_scale=w_planes[PACK * (c % GROUPS) : P, c // GROUPS, bank_cols[j]],
+                start=(c == 0),
+                stop=(c == PASSES - 1),
+            )
+
+        for c in range(PASSES - TAPER):
             for j in range(BANKS):
-                cols = slice(j * BANK, (j + 1) * BANK)
-                nc.tensor.matmul_mx(
-                    out=acc[j][:],
-                    lhsT=act_codes[:, c * P : (c + 1) * P].bitcast(FP8X4),
-                    lhsT_scale=act_planes[:, c * P : (c + 1) * P],
-                    rhs=w_words[c][:, cols].bitcast(FP8X4),
-                    rhs_scale=w_planes[PACK * g : P, o, cols],
-                    start=(c == 0),
-                    stop=(c == PASSES - 1),
-                )
-                if c == PASSES - 1:
-                    nc.vector.scalar_tensor_tensor(
-                        out=mem[:, cols], in0=acc[j][:], scalar=3.0, in1=leak[:, cols], op0=ALU.mult, op1=ALU.mult
-                    )
-                    nc.vector.tensor_tensor(out=mem[:, cols], in0=mem[:, cols], in1=rest[:, cols], op=ALU.add)
-                    nc.sync.dma_start(out=out[:, cols], in_=mem[:, cols])
+                mx_pass(c, j)
+        mem = keep.tile([P, NEURONS], F32)
+        for j in range(BANKS):
+            cols = bank_cols[j]
+            for c in range(PASSES - TAPER, PASSES):
+                mx_pass(c, j)
+            nc.vector.scalar_tensor_tensor(
+                out=mem[:, cols], in0=acc[j][:], scalar=3.0, in1=leak[:, cols], op0=ALU.mult, op1=ALU.mult
+            )
+            nc.vector.tensor_tensor(out=mem[:, cols], in0=mem[:, cols], in1=rest[:, cols], op=ALU.add)
+            nc.sync.dma_start(out=out[:, cols], in_=mem[:, cols])

@@ -24,7 +24,7 @@ BANK = 512
 BANKS = NEURONS // BANK
 WORDS = K_PASS // 2
 TAPER = 3
-SMALL_PER_LARGE = 2
+PIECE_WIDTHS = [BANK] * (BANKS - 1) + [BANK // 2] * 2
 
 TAU_M, TAU_ADP, BIAS = 0, 1, 2
 
@@ -54,64 +54,62 @@ def tile_snnlayer_pa_kernel(
     weight_words = (W_x2in_words, W_out2in_words, W_rec4in_words)
     weight_scales = (W_x2in_scales, W_out2in_scales, W_rec4in_scales)
     bank_cols = [slice(j * BANK, (j + 1) * BANK) for j in range(BANKS)]
+    piece_first = [sum(PIECE_WIDTHS[:i]) for i in range(len(PIECE_WIDTHS))]
+    piece_cols = [slice(first, first + width) for first, width in zip(piece_first, PIECE_WIDTHS)]
 
     with ExitStack() as ctx:
         keep = ctx.enter_context(tc.tile_pool(name="keep", bufs=1))
         acc_pool = ctx.enter_context(tc.psum_pool(name="acc", bufs=1))
-        bank_pool = ctx.enter_context(tc.psum_pool(name="bank", bufs=4))
-
-        small_loads = []
-        large_loads = []
+        bank_pool = ctx.enter_context(tc.psum_pool(name="bank", bufs=8 - len(PIECE_WIDTHS)))
+        ctx.enter_context(tc.manual_schedule())
 
         vec_rows = keep.tile([P, NEURONS], BF16)
         nc.vector.memset(vec_rows[:], 0.0)
-        small_loads.append((vec_rows[32:33, :], tau_adp_in.unsqueeze(0)))
-        small_loads.append((vec_rows[0:1, :], tau_m_in.unsqueeze(0)))
-        small_loads.append((vec_rows[64:65, :], b_x2in.unsqueeze(0)))
-        small_loads.append((vec_rows[65:66, :], b_rec4in.unsqueeze(0)))
-        small_loads.append((vec_rows[66:67, :], b_out2in.unsqueeze(0)))
+        nc.scalar.dma_start(out=vec_rows[0:1, :], in_=tau_m_in.unsqueeze(0))
+        nc.scalar.dma_start(out=vec_rows[64:65, :], in_=b_x2in.unsqueeze(0))
+        nc.scalar.dma_start(out=vec_rows[65:66, :], in_=b_rec4in.unsqueeze(0))
+        nc.scalar.dma_start(out=vec_rows[66:67, :], in_=b_out2in.unsqueeze(0))
+        nc.scalar.dma_start(out=vec_rows[32:33, :], in_=tau_adp_in.unsqueeze(0))
+
+        ident = keep.tile([P, P], F32)
+        make_identity(nc, ident[:])
 
         w_planes = keep.tile([P, OPERANDS, NEURONS], U8, align_bytes=64)
         nc.vector.memset(w_planes[:].bitcast(I32), 0)
         for o in range(OPERANDS):
             for quad in range(4):
-                small_loads.append(
-                    (
-                        w_planes[32 * quad : 32 * quad + 16, o, :].bitcast(I32),
-                        weight_scales[o][:, 4 * quad : 4 * quad + 4, :].bitcast(I32),
-                    )
+                nc.gpsimd.dma_start(
+                    out=w_planes[32 * quad : 32 * quad + 16, o, :].bitcast(F32),
+                    in_=weight_scales[o][:, 4 * quad : 4 * quad + 4, :].bitcast(F32),
                 )
+        issued = keep.tile([P, 1], F32)
+        nc.gpsimd.memset(issued[:], 1.0)
 
         acts = keep.tile([P, PASSES * K_PASS], BF16)
         spk_in = acts[:, 2 * FEATURES : 3 * FEATURES]
         b_last = keep.tile([P, NEURONS], BF16)
         mem_last = keep.tile([P, NEURONS], BF16)
-        large_loads.append((acts[:, 0:FEATURES], x_t))
-        large_loads.append((acts[:, FEATURES : 3 * FEATURES], spk_t))
-        large_loads.append((b_last[:], b_t_in))
-        large_loads.append((mem_last[:], mem_t_in))
+        nc.sync.dma_start(out=acts[:, 0:FEATURES], in_=x_t)
+        nc.sync.dma_start(out=acts[:, FEATURES : 3 * FEATURES], in_=spk_t)
+        nc.sync.dma_start(out=b_last[:], in_=b_t_in)
+        nc.sync.dma_start(out=mem_last[:], in_=mem_t_in)
 
         w_words = []
         for c in range(PASSES):
             w_words.append(keep.tile([P, NEURONS], U32, name="w_words_%d" % c, align_bytes=64))
 
-        def weight_load(c, first, width):
+        def load_weight_words(c, first, width):
             source = weight_words[c // GROUPS][c % GROUPS].rearrange("p n t -> p (n t)")
-            return (
-                w_words[c][:, first : first + width].bitcast(I32),
-                source[:, PACK * first : PACK * (first + width)].bitcast(I32),
+            nc.sync.dma_start(
+                out=w_words[c][:, first : first + width].bitcast(I32),
+                in_=source[:, PACK * first : PACK * (first + width)].bitcast(I32),
             )
 
         for c in range(PASSES - TAPER):
-            large_loads.append(weight_load(c, 0, NEURONS))
-        for j in range(BANKS):
+            load_weight_words(c, 0, NEURONS)
+        for first, width in zip(piece_first, PIECE_WIDTHS):
             for c in range(PASSES - TAPER, PASSES):
-                large_loads.append(weight_load(c, j * BANK, BANK))
-
-        for i, (destination, source) in enumerate(large_loads):
-            nc.sync.dma_start(out=destination, in_=source)
-            for small_destination, small_source in small_loads[SMALL_PER_LARGE * i : SMALL_PER_LARGE * (i + 1)]:
-                nc.sync.dma_start(out=small_destination, in_=small_source)
+                load_weight_words(c, first, width)
 
         pick = keep.tile([P, 3, P], BF16)
         nc.vector.memset(pick[:], 0.0)
@@ -119,8 +117,6 @@ def tile_snnlayer_pa_kernel(
         nc.vector.memset(pick[32:64, TAU_ADP, :], 1.0)
         nc.vector.memset(pick[64:128, BIAS, :], 1.0)
 
-        ident = keep.tile([P, P], F32)
-        make_identity(nc, ident[:])
         act_words = acts[:].bitcast(F32)
         grouped = keep.tile([P, PASSES, P, PACK], BF16, align_bytes=64)
         grouped_words = grouped[:].bitcast(F32)
@@ -155,30 +151,13 @@ def tile_snnlayer_pa_kernel(
             nc.tensor.matmul(spread[:], lhsT=pick[:, v, :], rhs=vec_rows[:, cols], start=True, stop=True)
             return spread
 
-        adapt = keep.tile([P, NEURONS], F32)
-        for cols in bank_cols:
-            nc.scalar.activation(out=adapt[:, cols], in_=spread_vector(TAU_ADP, cols)[:], func=ACT.Sigmoid)
-        spk_part = keep.tile([P, NEURONS], F32)
-        nc.scalar.activation(out=spk_part[:], in_=spk_in, func=ACT.Copy, bias=0.1, scale=1.8)
         decay = keep.tile([P, NEURONS], F32)
         leak = keep.tile([P, NEURONS], F32)
+        rest = keep.tile([P, NEURONS], F32)
         for cols in bank_cols:
             tau = spread_vector(TAU_M, cols)
             nc.scalar.activation(out=decay[:, cols], in_=tau[:], func=ACT.Sigmoid)
             nc.scalar.activation(out=leak[:, cols], in_=tau[:], func=ACT.Sigmoid, scale=-1.0)
-
-        thre = keep.tile([P, NEURONS], F32)
-        nc.vector.tensor_tensor(out=thre[:], in0=b_last[:], in1=spk_in, op=ALU.subtract)
-        nc.vector.tensor_tensor(out=thre[:], in0=thre[:], in1=adapt[:], op=ALU.mult)
-        nc.vector.scalar_tensor_tensor(
-            out=thre[:], in0=thre[:], scalar=1.8, in1=spk_part[:], op0=ALU.mult, op1=ALU.add
-        )
-        nc.vector.tensor_tensor(out=thre[:], in0=thre[:], in1=spk_in, op=ALU.mult)
-        kept = keep.tile([P, NEURONS], F32)
-        nc.vector.tensor_tensor(out=kept[:], in0=mem_last[:], in1=decay[:], op=ALU.mult)
-        nc.vector.tensor_tensor(out=kept[:], in0=kept[:], in1=thre[:], op=ALU.subtract)
-        rest = keep.tile([P, NEURONS], F32)
-        for cols in bank_cols:
             nc.vector.scalar_tensor_tensor(
                 out=rest[:, cols],
                 in0=spread_vector(BIAS, cols)[:],
@@ -187,33 +166,50 @@ def tile_snnlayer_pa_kernel(
                 op0=ALU.mult,
                 op1=ALU.mult,
             )
+        adapt = keep.tile([P, NEURONS], F32)
+        for cols in bank_cols:
+            nc.scalar.activation(out=adapt[:, cols], in_=spread_vector(TAU_ADP, cols)[:], func=ACT.Sigmoid)
+        spk_part = keep.tile([P, NEURONS], F32)
+        nc.scalar.activation(out=spk_part[:], in_=spk_in, func=ACT.Copy, bias=0.1, scale=1.8)
+
+        thre = keep.tile([P, NEURONS], F32)
+        nc.vector.scalar_tensor_tensor(
+            out=thre[:], in0=b_last[:], scalar=issued[:, 0:1], in1=spk_in, op0=ALU.mult, op1=ALU.subtract
+        )
+        kept = keep.tile([P, NEURONS], F32)
+        nc.vector.tensor_tensor(out=kept[:], in0=mem_last[:], in1=decay[:], op=ALU.mult)
+        nc.vector.tensor_tensor(out=thre[:], in0=thre[:], in1=adapt[:], op=ALU.mult)
+        nc.vector.scalar_tensor_tensor(
+            out=thre[:], in0=thre[:], scalar=1.8, in1=spk_part[:], op0=ALU.mult, op1=ALU.add
+        )
+        nc.vector.tensor_tensor(out=thre[:], in0=thre[:], in1=spk_in, op=ALU.mult)
+        nc.vector.tensor_tensor(out=kept[:], in0=kept[:], in1=thre[:], op=ALU.subtract)
         nc.vector.tensor_tensor(out=rest[:], in0=rest[:], in1=kept[:], op=ALU.add)
 
         acc = []
-        for j in range(BANKS):
-            acc.append(acc_pool.tile([P, BANK], F32, name="acc_%d" % j))
+        for i, width in enumerate(PIECE_WIDTHS):
+            acc.append(acc_pool.tile([P, width], F32, name="acc_%d" % i))
 
-        def mx_pass(c, j):
+        def mx_pass(c, i):
             nc.tensor.matmul_mx(
-                out=acc[j][:],
+                out=acc[i][:],
                 lhsT=act_codes[:, c * P : (c + 1) * P].bitcast(FP8X4),
                 lhsT_scale=act_planes[:, c * P : (c + 1) * P],
-                rhs=w_words[c][:, bank_cols[j]].bitcast(FP8X4),
-                rhs_scale=w_planes[PACK * (c % GROUPS) : P, c // GROUPS, bank_cols[j]],
+                rhs=w_words[c][:, piece_cols[i]].bitcast(FP8X4),
+                rhs_scale=w_planes[PACK * (c % GROUPS) : P, c // GROUPS, piece_cols[i]],
                 start=(c == 0),
                 stop=(c == PASSES - 1),
             )
 
         for c in range(PASSES - TAPER):
-            for j in range(BANKS):
-                mx_pass(c, j)
+            for i in range(len(PIECE_WIDTHS)):
+                mx_pass(c, i)
         mem = keep.tile([P, NEURONS], F32)
-        for j in range(BANKS):
-            cols = bank_cols[j]
+        for i, cols in enumerate(piece_cols):
             for c in range(PASSES - TAPER, PASSES):
-                mx_pass(c, j)
+                mx_pass(c, i)
             nc.vector.scalar_tensor_tensor(
-                out=mem[:, cols], in0=acc[j][:], scalar=3.0, in1=leak[:, cols], op0=ALU.mult, op1=ALU.mult
+                out=mem[:, cols], in0=acc[i][:], scalar=3.0, in1=leak[:, cols], op0=ALU.mult, op1=ALU.mult
             )
             nc.vector.tensor_tensor(out=mem[:, cols], in0=mem[:, cols], in1=rest[:, cols], op=ALU.add)
             nc.sync.dma_start(out=out[:, cols], in_=mem[:, cols])

@@ -82,9 +82,6 @@ def tile_snnlayer_pa_kernel(
                     out=w_planes[32 * quad : 32 * quad + 16, o, :].bitcast(F32),
                     in_=weight_scales[o][:, 4 * quad : 4 * quad + 4, :].bitcast(F32),
                 )
-        issued = keep.tile([P, 1], F32)
-        nc.gpsimd.memset(issued[:], 1.0)
-
         acts = keep.tile([P, PASSES * K_PASS], BF16)
         spk_in = acts[:, 2 * FEATURES : 3 * FEATURES]
         b_last = keep.tile([P, NEURONS], BF16)
@@ -146,6 +143,8 @@ def tile_snnlayer_pa_kernel(
                 in_=grouped[:, o * GROUPS : (o + 1) * GROUPS, :, :].rearrange("p g b t -> p (g b t)"),
             )
 
+        thre = keep.tile([P, NEURONS], F32)
+        nc.vector.tensor_tensor(out=thre[:], in0=b_last[:], in1=spk_in, op=ALU.subtract)
         def spread_vector(v, cols):
             spread = bank_pool.tile([P, BANK], F32, tag="bank")
             nc.tensor.matmul(spread[:], lhsT=pick[:, v, :], rhs=vec_rows[:, cols], start=True, stop=True)
@@ -172,10 +171,6 @@ def tile_snnlayer_pa_kernel(
         spk_part = keep.tile([P, NEURONS], F32)
         nc.scalar.activation(out=spk_part[:], in_=spk_in, func=ACT.Copy, bias=0.1, scale=1.8)
 
-        thre = keep.tile([P, NEURONS], F32)
-        nc.vector.scalar_tensor_tensor(
-            out=thre[:], in0=b_last[:], scalar=issued[:, 0:1], in1=spk_in, op0=ALU.mult, op1=ALU.subtract
-        )
         kept = keep.tile([P, NEURONS], F32)
         nc.vector.tensor_tensor(out=kept[:], in0=mem_last[:], in1=decay[:], op=ALU.mult)
         nc.vector.tensor_tensor(out=thre[:], in0=thre[:], in1=adapt[:], op=ALU.mult)

@@ -23,7 +23,7 @@ PASSES = OPERANDS * GROUPS
 BANK = 512
 BANKS = NEURONS // BANK
 WORDS = K_PASS // 2
-TAPER = 3
+TAPER = 4
 PIECE_WIDTHS = [BANK] * (BANKS - 1) + [BANK // 2] * 2
 
 TAU_M, TAU_ADP, BIAS = 0, 1, 2

from contextlib import ExitStack

import concourse.mybir as mybir
from concourse.masks import make_identity

F32 = mybir.dt.float32
BF16 = mybir.dt.bfloat16
I32 = mybir.dt.int32
U32 = mybir.dt.uint32
U8 = mybir.dt.uint8
FP8X4 = mybir.dt.float8_e4m3fn_x4
ALU = mybir.AluOpType
ACT = mybir.ActivationFunctionType

P = 128
PACK = 4
K_PASS = P * PACK
FEATURES = 2048
NEURONS = 2048
OPERANDS = 3
GROUPS = FEATURES // K_PASS
PASSES = OPERANDS * GROUPS
BANK = 512
BANKS = NEURONS // BANK
WORDS = K_PASS // 2
TAPER = 4
PIECE_WIDTHS = [BANK] * (BANKS - 1) + [BANK // 2] * 2

TAU_M, TAU_ADP, BIAS = 0, 1, 2

FLOPS = 2 * P * OPERANDS * FEATURES * NEURONS


def tile_snnlayer_pa_kernel(
    tc,
    x_t,
    spk_t,
    mem_t_in,
    b_t_in,
    W_x2in_words,
    W_x2in_scales,
    b_x2in,
    W_rec4in_words,
    W_rec4in_scales,
    b_rec4in,
    W_out2in_words,
    W_out2in_scales,
    b_out2in,
    tau_adp_in,
    tau_m_in,
    out,
):
    nc = tc.nc
    weight_words = (W_x2in_words, W_out2in_words, W_rec4in_words)
    weight_scales = (W_x2in_scales, W_out2in_scales, W_rec4in_scales)
    bank_cols = [slice(j * BANK, (j + 1) * BANK) for j in range(BANKS)]
    piece_first = [sum(PIECE_WIDTHS[:i]) for i in range(len(PIECE_WIDTHS))]
    piece_cols = [slice(first, first + width) for first, width in zip(piece_first, PIECE_WIDTHS)]

    with ExitStack() as ctx:
        keep = ctx.enter_context(tc.tile_pool(name="keep", bufs=1))
        acc_pool = ctx.enter_context(tc.psum_pool(name="acc", bufs=1))
        bank_pool = ctx.enter_context(tc.psum_pool(name="bank", bufs=8 - len(PIECE_WIDTHS)))
        ctx.enter_context(tc.manual_schedule())

        vec_rows = keep.tile([P, NEURONS], BF16)
        nc.vector.memset(vec_rows[:], 0.0)
        nc.scalar.dma_start(out=vec_rows[0:1, :], in_=tau_m_in.unsqueeze(0))
        nc.scalar.dma_start(out=vec_rows[64:65, :], in_=b_x2in.unsqueeze(0))
        nc.scalar.dma_start(out=vec_rows[65:66, :], in_=b_rec4in.unsqueeze(0))
        nc.scalar.dma_start(out=vec_rows[66:67, :], in_=b_out2in.unsqueeze(0))
        nc.scalar.dma_start(out=vec_rows[32:33, :], in_=tau_adp_in.unsqueeze(0))

        ident = keep.tile([P, P], F32)
        make_identity(nc, ident[:])

        w_planes = keep.tile([P, OPERANDS, NEURONS], U8, align_bytes=64)
        nc.vector.memset(w_planes[:].bitcast(I32), 0)
        for o in range(OPERANDS):
            for quad in range(4):
                nc.gpsimd.dma_start(
                    out=w_planes[32 * quad : 32 * quad + 16, o, :].bitcast(F32),
                    in_=weight_scales[o][:, 4 * quad : 4 * quad + 4, :].bitcast(F32),
                )
        acts = keep.tile([P, PASSES * K_PASS], BF16)
        spk_in = acts[:, 2 * FEATURES : 3 * FEATURES]
        b_last = keep.tile([P, NEURONS], BF16)
        mem_last = keep.tile([P, NEURONS], BF16)
        nc.sync.dma_start(out=acts[:, 0:FEATURES], in_=x_t)
        nc.sync.dma_start(out=acts[:, FEATURES : 3 * FEATURES], in_=spk_t)
        nc.sync.dma_start(out=b_last[:], in_=b_t_in)
        nc.sync.dma_start(out=mem_last[:], in_=mem_t_in)

        w_words = []
        for c in range(PASSES):
            w_words.append(keep.tile([P, NEURONS], U32, name="w_words_%d" % c, align_bytes=64))

        def load_weight_words(c, first, width):
            source = weight_words[c // GROUPS][c % GROUPS].rearrange("p n t -> p (n t)")
            nc.sync.dma_start(
                out=w_words[c][:, first : first + width].bitcast(I32),
                in_=source[:, PACK * first : PACK * (first + width)].bitcast(I32),
            )

        for c in range(PASSES - TAPER):
            load_weight_words(c, 0, NEURONS)
        for first, width in zip(piece_first, PIECE_WIDTHS):
            for c in range(PASSES - TAPER, PASSES):
                load_weight_words(c, first, width)

        pick = keep.tile([P, 3, P], BF16)
        nc.vector.memset(pick[:], 0.0)
        nc.vector.memset(pick[0:32, TAU_M, :], 1.0)
        nc.vector.memset(pick[32:64, TAU_ADP, :], 1.0)
        nc.vector.memset(pick[64:128, BIAS, :], 1.0)

        act_words = acts[:].bitcast(F32)
        grouped = keep.tile([P, PASSES, P, PACK], BF16, align_bytes=64)
        grouped_words = grouped[:].bitcast(F32)
        act_codes = keep.tile([P, PASSES * P], U32, align_bytes=64)
        act_planes = keep.tile([P, PASSES * P], U8, align_bytes=64)
        for pair in range(PASSES // 2):
            flipped = bank_pool.tile([P, 2, 2, P], F32, tag="bank")
            for h in range(2):
                c = 2 * pair + h
                for u in range(2):
                    nc.tensor.transpose(
                        flipped[:, h, u, :],
                        act_words[:, c * WORDS + u : (c + 1) * WORDS : 2],
                        ident[:],
                    )
            target = grouped_words[:, 2 * pair : 2 * pair + 2, :, :]
            permuted = flipped[:].rearrange("p h u b -> p h b u")
            if pair % 2 == 0:
                nc.vector.tensor_copy(out=target, in_=permuted)
            else:
                nc.scalar.copy(out=target, in_=permuted)
        for o in range(OPERANDS):
            cols = slice(o * GROUPS * P, (o + 1) * GROUPS * P)
            nc.vector.quantize_mx(
                out=act_codes[:, cols].bitcast(FP8X4),
                scales=act_planes[:, cols],
                in_=grouped[:, o * GROUPS : (o + 1) * GROUPS, :, :].rearrange("p g b t -> p (g b t)"),
            )

        thre = keep.tile([P, NEURONS], F32)
        nc.vector.tensor_tensor(out=thre[:], in0=b_last[:], in1=spk_in, op=ALU.subtract)
        def spread_vector(v, cols):
            spread = bank_pool.tile([P, BANK], F32, tag="bank")
            nc.tensor.matmul(spread[:], lhsT=pick[:, v, :], rhs=vec_rows[:, cols], start=True, stop=True)
            return spread

        decay = keep.tile([P, NEURONS], F32)
        leak = keep.tile([P, NEURONS], F32)
        rest = keep.tile([P, NEURONS], F32)
        for cols in bank_cols:
            tau = spread_vector(TAU_M, cols)
            nc.scalar.activation(out=decay[:, cols], in_=tau[:], func=ACT.Sigmoid)
            nc.scalar.activation(out=leak[:, cols], in_=tau[:], func=ACT.Sigmoid, scale=-1.0)
            nc.vector.scalar_tensor_tensor(
                out=rest[:, cols],
                in0=spread_vector(BIAS, cols)[:],
                scalar=3.0,
                in1=leak[:, cols],
                op0=ALU.mult,
                op1=ALU.mult,
            )
        adapt = keep.tile([P, NEURONS], F32)
        for cols in bank_cols:
            nc.scalar.activation(out=adapt[:, cols], in_=spread_vector(TAU_ADP, cols)[:], func=ACT.Sigmoid)
        spk_part = keep.tile([P, NEURONS], F32)
        nc.scalar.activation(out=spk_part[:], in_=spk_in, func=ACT.Copy, bias=0.1, scale=1.8)

        kept = keep.tile([P, NEURONS], F32)
        nc.vector.tensor_tensor(out=kept[:], in0=mem_last[:], in1=decay[:], op=ALU.mult)
        nc.vector.tensor_tensor(out=thre[:], in0=thre[:], in1=adapt[:], op=ALU.mult)
        nc.vector.scalar_tensor_tensor(
            out=thre[:], in0=thre[:], scalar=1.8, in1=spk_part[:], op0=ALU.mult, op1=ALU.add
        )
        nc.vector.tensor_tensor(out=thre[:], in0=thre[:], in1=spk_in, op=ALU.mult)
        nc.vector.tensor_tensor(out=kept[:], in0=kept[:], in1=thre[:], op=ALU.subtract)
        nc.vector.tensor_tensor(out=rest[:], in0=rest[:], in1=kept[:], op=ALU.add)

        acc = []
        for i, width in enumerate(PIECE_WIDTHS):
            acc.append(acc_pool.tile([P, width], F32, name="acc_%d" % i))

        def mx_pass(c, i):
            nc.tensor.matmul_mx(
                out=acc[i][:],
                lhsT=act_codes[:, c * P : (c + 1) * P].bitcast(FP8X4),
                lhsT_scale=act_planes[:, c * P : (c + 1) * P],
                rhs=w_words[c][:, piece_cols[i]].bitcast(FP8X4),
                rhs_scale=w_planes[PACK * (c % GROUPS) : P, c // GROUPS, piece_cols[i]],
                start=(c == 0),
                stop=(c == PASSES - 1),
            )

        for c in range(PASSES - TAPER):
            for i in range(len(PIECE_WIDTHS)):
                mx_pass(c, i)
        mem = keep.tile([P, NEURONS], F32)
        for i, cols in enumerate(piece_cols):
            for c in range(PASSES - TAPER, PASSES):
                mx_pass(c, i)
            nc.vector.scalar_tensor_tensor(
                out=mem[:, cols], in0=acc[i][:], scalar=3.0, in1=leak[:, cols], op0=ALU.mult, op1=ALU.mult
            )
            nc.vector.tensor_tensor(out=mem[:, cols], in0=mem[:, cols], in1=rest[:, cols], op=ALU.add)
            nc.sync.dma_start(out=out[:, cols], in_=mem[:, cols])
